import numpy as np
import ml_dtypes


def mxq(x, axis, fmt="e4m3"):
    dtype, down = {"e4m3": (ml_dtypes.float8_e4m3fn, 7), "e5m2": (ml_dtypes.float8_e5m2, 14)}[fmt]
    v = np.moveaxis(np.asarray(x, np.float32).astype(ml_dtypes.bfloat16).astype(np.float64), axis, -1)
    blocks = v.reshape(v.shape[:-1] + (-1, 32))
    amax = np.abs(blocks).max(-1, keepdims=True)
    byte = np.maximum(np.where(amax > 0, np.frexp(amax)[1] - 1 + 127, 0) - down, 1)
    scale = np.exp2(byte - 127.0)
    codes = (blocks / scale).astype(np.float32).astype(dtype).astype(np.float64)
    return np.moveaxis((codes * scale).reshape(v.shape), -1, axis)


WIDE = False


def mx_kscale(k):
    if not WIDE:
        return np.ones(k)
    levels = np.array([20, -20, 10, -10, 0])
    a = np.random.permutation(np.resize(levels, k // 512 * 4)).reshape(k // 512, 4)
    idx = np.arange(k)
    return np.exp2(a[idx // 512, idx % 128 // 32])


BF16 = ml_dtypes.bfloat16


def bf(x):
    return np.asarray(x, np.float32).astype(BF16)


def f64(x):
    return np.asarray(x).astype(np.float64)


N, M0, D0, M1, D1, M2, D2 = 1536, 512, 1, 512, 3, 256, 5
IRREPS = [(M0, D0), (M1, D1), (M2, D2)]
IN_DIM = sum(m * d for m, d in IRREPS)
OFF1 = M0 * D0
K1 = D1 * N


def _block1(a):
    return a[:, OFF1:OFF1 + M1 * D1].reshape(N, M1, D1).transpose(2, 0, 1).reshape(K1, M1)


def setup_inputs():
    s = mx_kscale(K1).reshape(D1, N)
    sx = np.ones((N, IN_DIM))
    sx[:, OFF1:OFF1 + M1 * D1] = np.tile(s.T, (1, M1))
    x = np.random.standard_normal((N, IN_DIM)) * sx
    w0 = np.random.standard_normal((M0, M0)) * 0.4
    w1 = np.random.standard_normal((M1, M1)) * 0.4
    w2 = np.random.standard_normal((M2, M2)) * 0.4
    g = np.random.standard_normal((N, IN_DIM)) * np.exp2(np.random.randint(-12, 1, (N, 1))) / sx
    return {"x": bf(x), "w0": bf(w0), "w1": bf(w1), "w2": bf(w2), "grad_out": bf(g)}


def reference(x, w0, w1, w2, grad_out):
    xb = _block1(f64(x))
    gb = _block1(f64(grad_out))
    p = mxq(xb, 0, "e4m3").T @ mxq(gb, 0, "e5m2")
    return (1.0 / np.sqrt(M1)) * p

@@ -1,0 +1,131 @@
+from contextlib import ExitStack
+import math
+
+import concourse.mybir as mybir
+
+BF16 = mybir.dt.bfloat16
+F32 = mybir.dt.float32
+U32 = mybir.dt.uint32
+U8 = mybir.dt.uint8
+E4M3X4 = mybir.dt.float8_e4m3fn_x4
+E5M2X4 = mybir.dt.float8_e5m2_x4
+
+P = 128
+PACK = 4
+K_PASS = P * PACK
+TOKENS = 1536
+MUL = 512
+DIM = 3
+OFF = 512
+CHUNKS = TOKENS // K_PASS
+M_TILE = 128
+M_TILES = MUL // M_TILE
+PIECE = 256
+PART = 128
+
+FLOPS = 2 * DIM * TOKENS * MUL * MUL
+BYTES = 2 * TOKENS * DIM * MUL * 2 + MUL * MUL * 4
+
+
+def tile_linear_kernel(tc, x, w0, w1, w2, grad_out, out):
+    nc = tc.nc
+    scale = 1.0 / math.sqrt(MUL)
+    with ExitStack() as ctx:
+        raw_pool = ctx.enter_context(tc.tile_pool(name="raw", bufs=1))
+        grp_pool = ctx.enter_context(tc.tile_pool(name="grp", bufs=1))
+        mx_pool = ctx.enter_context(tc.tile_pool(name="mx", bufs=1))
+        res_pool = ctx.enter_context(tc.tile_pool(name="res", bufs=1))
+        psum = ctx.enter_context(tc.psum_pool(name="acc", bufs=1))
+        ctx.enter_context(tc.manual_schedule())
+
+        sources = {"x": x, "g": grad_out}
+        formats = {"x": E4M3X4, "g": E5M2X4}
+        codes = {}
+        planes = {}
+        for o in ("x", "g"):
+            for c in range(CHUNKS):
+                codes[(o, c)] = mx_pool.tile([P, DIM, MUL], U32, name="codes_%s%d" % (o, c), align_bytes=64)
+                planes[(o, c)] = mx_pool.tile([P, DIM, MUL], U8, name="planes_%s%d" % (o, c), align_bytes=64)
+        acc = [psum.tile([P, MUL], F32, name="acc%d" % m) for m in range(M_TILES)]
+
+        warm = res_pool.tile([P, 8], F32, name="warm")
+        nc.vector.memset(warm[:], 0.0)
+        nc.scalar.mul(warm[:], warm[:], 1.0)
+
+        order = [("x", 0), ("g", 0), ("x", 1), ("g", 1), ("g", 2), ("x", 2)]
+        pieces = [(o, c, u0) for (o, c) in order for u0 in range(0, MUL, PIECE)]
+
+        raw = []
+        for (o, c, u0) in pieces:
+            t = raw_pool.tile([P, PACK, DIM * PIECE], BF16, name="raw_%s%d_%d" % (o, c, u0))
+            rows = sources[o][c * K_PASS:(c + 1) * K_PASS, OFF + DIM * u0:OFF + DIM * (u0 + PIECE)]
+            nc.sync.dma_start(out=t[:], in_=rows.rearrange("(p j) w -> p j w", j=PACK))
+            raw.append(t)
+
+        def regroup(k, half):
+            o, c, u0 = pieces[k]
+            g = grp_pool.tile([P, DIM, PART, PACK], BF16, name="grp_%d_%d" % (k, half), align_bytes=64)
+            src = raw[k][:].rearrange("p j (u i) -> p u j i", i=DIM)[:, half * PART:(half + 1) * PART, :, :]
+            dst = g[:].rearrange("p i u j -> p u j i")
+            if half == 0:
+                nc.vector.tensor_copy(out=dst, in_=src)
+            else:
+                nc.scalar.copy(out=dst, in_=src)
+            return g
+
+        def quantise(k, half, g):
+            o, c, u0 = pieces[k]
+            a = u0 + half * PART
+            for i in range(DIM):
+                nc.vector.quantize_mx(
+                    out=codes[(o, c)][:, i, a:a + PART].bitcast(formats[o]),
+                    scales=planes[(o, c)][:, i, a:a + PART],
+                    in_=g[:, i, :, :].rearrange("p u j -> p (u j)"),
+                )
+
+        def passes(c, m):
+            cols = slice(m * M_TILE, (m + 1) * M_TILE)
+            for i in range(DIM):
+                nc.tensor.matmul_mx(
+                    out=acc[m][:],
+                    lhsT=codes[("x", c)][:, i, cols].bitcast(E4M3X4),
+                    lhsT_scale=planes[("x", c)][:, i, cols],
+                    rhs=codes[("g", c)][:, i, :].bitcast(E5M2X4),
+                    rhs_scale=planes[("g", c)][:, i, :],
+                    start=(c == 0 and i == 0),
+                    stop=(c == CHUNKS - 1 and i == DIM - 1),
+                )
+
+        def finish(m):
+            res = res_pool.tile([P, MUL], F32, name="res%d" % m)
+            if m == M_TILES - 1:
+                nc.vector.tensor_scalar_mul(out=res[:], in0=acc[m][:], scalar1=scale)
+            else:
+                nc.scalar.mul(res[:], acc[m][:], scale)
+            nc.sync.dma_start(out=out[m * M_TILE:(m + 1) * M_TILE, :], in_=res[:])
+
+        n = len(pieces)
+        last = CHUNKS - 1
+        late = None
+        for k in range(n + 1):
+            if k < n:
+                g0 = regroup(k, 0)
+                g1 = regroup(k, 1)
+            if late is not None:
+                quantise(k - 1, 1, late)
+                o, c, u0 = pieces[k - 1]
+                if c < last and o == "g" and u0 + PIECE == MUL:
+                    for m in range(M_TILES):
+                        passes(c, m)
+                if c == last and o == "x":
+                    m = u0 // M_TILE + 1
+                    passes(c, m)
+                    if k == n:
+                        for mm in range(M_TILES):
+                            finish(mm)
+            if k < n:
+                quantise(k, 0, g0)
+                o, c, u0 = pieces[k]
+                if c == last and o == "x":
+                    passes(c, u0 // M_TILE)
+                late = g1

@@ -20,11 +20,18 @@ OFF = 512
 CHUNKS = TOKENS // K_PASS
 M_TILE = 128
 M_TILES = MUL // M_TILE
-PIECE = 256
-PART = 128
 
 FLOPS = 2 * DIM * TOKENS * MUL * MUL
 BYTES = 2 * TOKENS * DIM * MUL * 2 + MUL * MUL * 4
+
+PIECES = [
+    ("x", 0, 0, 256, 128), ("x", 0, 256, 256, 128),
+    ("g", 0, 0, 256, 128), ("g", 0, 256, 256, 128),
+    ("x", 1, 0, 256, 128), ("x", 1, 256, 256, 128),
+    ("g", 1, 0, 256, 128), ("g", 1, 256, 256, 128),
+    ("g", 2, 0, 256, 128), ("g", 2, 256, 256, 128),
+    ("x", 2, 0, 128, 64), ("x", 2, 128, 128, 64), ("x", 2, 256, 128, 64), ("x", 2, 384, 128, 64),
+]
 
 
 def tile_linear_kernel(tc, x, w0, w1, w2, grad_out, out):
@@ -42,90 +49,96 @@ def tile_linear_kernel(tc, x, w0, w1, w2, grad_out, out):
         formats = {"x": E4M3X4, "g": E5M2X4}
         codes = {}
         planes = {}
-        for o in ("x", "g"):
-            for c in range(CHUNKS):
-                codes[(o, c)] = mx_pool.tile([P, DIM, MUL], U32, name="codes_%s%d" % (o, c), align_bytes=64)
-                planes[(o, c)] = mx_pool.tile([P, DIM, MUL], U8, name="planes_%s%d" % (o, c), align_bytes=64)
+        for c in range(CHUNKS):
+            for i in range(DIM):
+                codes[("g", c, i)] = mx_pool.tile([P, MUL], U32, name="gc_%d_%d" % (c, i), align_bytes=64)
+                planes[("g", c, i)] = mx_pool.tile([P, MUL], U8, name="gs_%d_%d" % (c, i), align_bytes=64)
         acc = [psum.tile([P, MUL], F32, name="acc%d" % m) for m in range(M_TILES)]
 
         warm = res_pool.tile([P, 8], F32, name="warm")
         nc.vector.memset(warm[:], 0.0)
         nc.scalar.mul(warm[:], warm[:], 1.0)
 
-        order = [("x", 0), ("g", 0), ("x", 1), ("g", 1), ("g", 2), ("x", 2)]
-        pieces = [(o, c, u0) for (o, c) in order for u0 in range(0, MUL, PIECE)]
-
         raw = []
-        for (o, c, u0) in pieces:
-            t = raw_pool.tile([P, PACK, DIM * PIECE], BF16, name="raw_%s%d_%d" % (o, c, u0))
-            rows = sources[o][c * K_PASS:(c + 1) * K_PASS, OFF + DIM * u0:OFF + DIM * (u0 + PIECE)]
+        for (o, c, u0, width, v_share) in PIECES:
+            t = raw_pool.tile([P, PACK, DIM * width], BF16, name="raw_%s%d_%d" % (o, c, u0))
+            rows = sources[o][c * K_PASS:(c + 1) * K_PASS, OFF + DIM * u0:OFF + DIM * (u0 + width)]
             nc.sync.dma_start(out=t[:], in_=rows.rearrange("(p j) w -> p j w", j=PACK))
             raw.append(t)
 
-        def regroup(k, half):
-            o, c, u0 = pieces[k]
-            g = grp_pool.tile([P, DIM, PART, PACK], BF16, name="grp_%d_%d" % (k, half), align_bytes=64)
-            src = raw[k][:].rearrange("p j (u i) -> p u j i", i=DIM)[:, half * PART:(half + 1) * PART, :, :]
+        def regroup(k):
+            o, c, u0, width, v_share = PIECES[k]
+            g = grp_pool.tile([P, DIM, width, PACK], BF16, name="grp_%d" % k, align_bytes=64)
+            src = raw[k][:].rearrange("p j (u i) -> p u j i", i=DIM)
             dst = g[:].rearrange("p i u j -> p u j i")
-            if half == 0:
-                nc.vector.tensor_copy(out=dst, in_=src)
-            else:
-                nc.scalar.copy(out=dst, in_=src)
+            nc.vector.tensor_copy(out=dst[:, 0:v_share, :, :], in_=src[:, 0:v_share, :, :])
+            nc.scalar.copy(out=dst[:, v_share:width, :, :], in_=src[:, v_share:width, :, :])
             return g
 
-        def quantise(k, half, g):
-            o, c, u0 = pieces[k]
-            a = u0 + half * PART
+        def quantise(k, g):
+            o, c, u0, width, v_share = PIECES[k]
             for i in range(DIM):
+                if o == "x":
+                    codes[(o, c, i, u0)] = mx_pool.tile([P, width], U32, name="xc_%d_%d_%d" % (c, i, u0), align_bytes=64)
+                    planes[(o, c, i, u0)] = mx_pool.tile([P, width], U8, name="xs_%d_%d_%d" % (c, i, u0), align_bytes=64)
+                    words = codes[(o, c, i, u0)][:, :]
+                    plane = planes[(o, c, i, u0)][:, :]
+                else:
+                    words = codes[(o, c, i)][:, u0:u0 + width]
+                    plane = planes[(o, c, i)][:, u0:u0 + width]
                 nc.vector.quantize_mx(
-                    out=codes[(o, c)][:, i, a:a + PART].bitcast(formats[o]),
-                    scales=planes[(o, c)][:, i, a:a + PART],
+                    out=words.bitcast(formats[o]),
+                    scales=plane,
                     in_=g[:, i, :, :].rearrange("p u j -> p (u j)"),
                 )
 
-        def passes(c, m):
-            cols = slice(m * M_TILE, (m + 1) * M_TILE)
-            for i in range(DIM):
-                nc.tensor.matmul_mx(
-                    out=acc[m][:],
-                    lhsT=codes[("x", c)][:, i, cols].bitcast(E4M3X4),
-                    lhsT_scale=planes[("x", c)][:, i, cols],
-                    rhs=codes[("g", c)][:, i, :].bitcast(E5M2X4),
-                    rhs_scale=planes[("g", c)][:, i, :],
-                    start=(c == 0 and i == 0),
-                    stop=(c == CHUNKS - 1 and i == DIM - 1),
-                )
+        def passes(c, u0, width):
+            for m in range(u0 // M_TILE, (u0 + width) // M_TILE):
+                cols = slice(m * M_TILE - u0, (m + 1) * M_TILE - u0)
+                for i in range(DIM):
+                    nc.tensor.matmul_mx(
+                        out=acc[m][:],
+                        lhsT=codes[("x", c, i, u0)][:, cols].bitcast(E4M3X4),
+                        lhsT_scale=planes[("x", c, i, u0)][:, cols],
+                        rhs=codes[("g", c, i)][:, :].bitcast(E5M2X4),
+                        rhs_scale=planes[("g", c, i)][:, :],
+                        start=(c == 0 and i == 0),
+                        stop=(c == CHUNKS - 1 and i == DIM - 1),
+                    )
 
         def finish(m):
-            res = res_pool.tile([P, MUL], F32, name="res%d" % m)
-            if m == M_TILES - 1:
-                nc.vector.tensor_scalar_mul(out=res[:], in0=acc[m][:], scalar1=scale)
-            else:
+            rows = out[m * M_TILE:(m + 1) * M_TILE, :]
+            if m < M_TILES - 1:
+                res = res_pool.tile([P, MUL], F32, name="res%d" % m)
                 nc.scalar.mul(res[:], acc[m][:], scale)
-            nc.sync.dma_start(out=out[m * M_TILE:(m + 1) * M_TILE, :], in_=res[:])
+                nc.sync.dma_start(out=rows, in_=res[:])
+            else:
+                half = MUL // 2
+                for h in range(2):
+                    res = res_pool.tile([P, half], F32, name="res%d_%d" % (m, h))
+                    nc.vector.tensor_scalar_mul(out=res[:], in0=acc[m][:, h * half:(h + 1) * half], scalar1=scale)
+                    nc.sync.dma_start(out=rows[:, h * half:(h + 1) * half], in_=res[:])
 
-        n = len(pieces)
-        last = CHUNKS - 1
-        late = None
+        n = len(PIECES)
+        waiting = []
+        g_done = {}
+        grouped = {}
         for k in range(n + 1):
             if k < n:
-                g0 = regroup(k, 0)
-                g1 = regroup(k, 1)
-            if late is not None:
-                quantise(k - 1, 1, late)
-                o, c, u0 = pieces[k - 1]
-                if c < last and o == "g" and u0 + PIECE == MUL:
-                    for m in range(M_TILES):
-                        passes(c, m)
-                if c == last and o == "x":
-                    m = u0 // M_TILE + 1
-                    passes(c, m)
-                    if k == n:
-                        for mm in range(M_TILES):
-                            finish(mm)
-            if k < n:
-                quantise(k, 0, g0)
-                o, c, u0 = pieces[k]
-                if c == last and o == "x":
-                    passes(c, u0 // M_TILE)
-                late = g1
+                grouped[k] = regroup(k)
+            if k > 0:
+                o, c, u0, width, v_share = PIECES[k - 1]
+                quantise(k - 1, grouped[k - 1])
+                if o == "g":
+                    g_done[c] = g_done.get(c, 0) + width
+                else:
+                    waiting.append((c, u0, width))
+                still = []
+                for (cc, uu, ww) in waiting:
+                    if g_done.get(cc, 0) == MUL:
+                        passes(cc, uu, ww)
+                    else:
+                        still.append((cc, uu, ww))
+                waiting = still
+        for m in range(M_TILES):
+            finish(m)

@@ -25,12 +25,12 @@ FLOPS = 2 * DIM * TOKENS * MUL * MUL
 BYTES = 2 * TOKENS * DIM * MUL * 2 + MUL * MUL * 4
 
 PIECES = [
-    ("x", 0, 0, 256, 128), ("x", 0, 256, 256, 128),
-    ("g", 0, 0, 256, 128), ("g", 0, 256, 256, 128),
-    ("x", 1, 0, 256, 128), ("x", 1, 256, 256, 128),
-    ("g", 1, 0, 256, 128), ("g", 1, 256, 256, 128),
-    ("g", 2, 0, 256, 128), ("g", 2, 256, 256, 128),
-    ("x", 2, 0, 128, 64), ("x", 2, 128, 128, 64), ("x", 2, 256, 128, 64), ("x", 2, 384, 128, 64),
+    ("x", 0, 0, 256, 136), ("x", 0, 256, 256, 136),
+    ("g", 0, 0, 256, 136), ("g", 0, 256, 256, 136),
+    ("x", 1, 0, 256, 136), ("x", 1, 256, 256, 136),
+    ("g", 1, 0, 256, 136), ("g", 1, 256, 256, 136),
+    ("g", 2, 0, 256, 136), ("g", 2, 256, 256, 136),
+    ("x", 2, 0, 128, 68), ("x", 2, 128, 128, 68), ("x", 2, 256, 128, 68), ("x", 2, 384, 128, 68),
 ]
 
 

@@ -25,12 +25,17 @@ FLOPS = 2 * DIM * TOKENS * MUL * MUL
 BYTES = 2 * TOKENS * DIM * MUL * 2 + MUL * MUL * 4
 
 PIECES = [
-    ("x", 0, 0, 256, 136), ("x", 0, 256, 256, 136),
-    ("g", 0, 0, 256, 136), ("g", 0, 256, 256, 136),
-    ("x", 1, 0, 256, 136), ("x", 1, 256, 256, 136),
-    ("g", 1, 0, 256, 136), ("g", 1, 256, 256, 136),
-    ("g", 2, 0, 256, 136), ("g", 2, 256, 256, 136),
-    ("x", 2, 0, 128, 68), ("x", 2, 128, 128, 68), ("x", 2, 256, 128, 68), ("x", 2, 384, 128, 68),
+    ("x", 0, 0, 256, 128), ("x", 0, 256, 256, 128),
+    ("g", 0, 0, 256, 128), ("g", 0, 256, 256, 128),
+    ("x", 1, 0, 256, 128), ("x", 1, 256, 256, 128),
+    ("g", 1, 0, 256, 128), ("g", 1, 256, 256, 128),
+    ("g", 2, 0, 256, 128), ("g", 2, 256, 256, 128),
+    ("x", 2, 0, 128, 64), ("x", 2, 128, 128, 64), ("x", 2, 256, 128, 64), ("x", 2, 384, 128, 64),
+]
+
+LOADS = [
+    ("x", 0, 0, 512), ("g", 0, 0, 512), ("x", 1, 0, 512), ("g", 1, 0, 512), ("g", 2, 0, 512),
+    ("x", 2, 0, 128), ("x", 2, 128, 128), ("x", 2, 256, 128), ("x", 2, 384, 128),
 ]
 
 
@@ -59,20 +64,23 @@ def tile_linear_kernel(tc, x, w0, w1, w2, grad_out, out):
         nc.vector.memset(warm[:], 0.0)
         nc.scalar.mul(warm[:], warm[:], 1.0)
 
-        raw = []
-        for (o, c, u0, width, v_share) in PIECES:
+        raw = {}
+        for (o, c, u0, width) in LOADS:
             t = raw_pool.tile([P, PACK, DIM * width], BF16, name="raw_%s%d_%d" % (o, c, u0))
             rows = sources[o][c * K_PASS:(c + 1) * K_PASS, OFF + DIM * u0:OFF + DIM * (u0 + width)]
             nc.sync.dma_start(out=t[:], in_=rows.rearrange("(p j) w -> p j w", j=PACK))
-            raw.append(t)
+            for (oo, cc, uu, ww, vv) in PIECES:
+                if oo == o and cc == c and u0 <= uu and uu + ww <= u0 + width:
+                    raw[(oo, cc, uu)] = (t, uu - u0)
 
         def regroup(k):
             o, c, u0, width, v_share = PIECES[k]
             g = grp_pool.tile([P, DIM, width, PACK], BF16, name="grp_%d" % k, align_bytes=64)
-            src = raw[k][:].rearrange("p j (u i) -> p u j i", i=DIM)
+            t, first = raw[(o, c, u0)]
+            src = t[:].rearrange("p j (u i) -> p u j i", i=DIM)
             dst = g[:].rearrange("p i u j -> p u j i")
-            nc.vector.tensor_copy(out=dst[:, 0:v_share, :, :], in_=src[:, 0:v_share, :, :])
-            nc.scalar.copy(out=dst[:, v_share:width, :, :], in_=src[:, v_share:width, :, :])
+            nc.vector.tensor_copy(out=dst[:, 0:v_share, :, :], in_=src[:, first:first + v_share, :, :])
+            nc.scalar.copy(out=dst[:, v_share:width, :, :], in_=src[:, first + v_share:first + width, :, :])
             return g
 
         def quantise(k, g):

@@ -20,22 +20,14 @@ OFF = 512
 CHUNKS = TOKENS // K_PASS
 M_TILE = 128
 M_TILES = MUL // M_TILE
+RUN = 8
 
 FLOPS = 2 * DIM * TOKENS * MUL * MUL
 BYTES = 2 * TOKENS * DIM * MUL * 2 + MUL * MUL * 4
 
-PIECES = [
-    ("x", 0, 0, 256, 128), ("x", 0, 256, 256, 128),
-    ("g", 0, 0, 256, 128), ("g", 0, 256, 256, 128),
-    ("x", 1, 0, 256, 128), ("x", 1, 256, 256, 128),
-    ("g", 1, 0, 256, 128), ("g", 1, 256, 256, 128),
-    ("g", 2, 0, 256, 128), ("g", 2, 256, 256, 128),
-    ("x", 2, 0, 128, 64), ("x", 2, 128, 128, 64), ("x", 2, 256, 128, 64), ("x", 2, 384, 128, 64),
-]
-
 LOADS = [
-    ("x", 0, 0, 512), ("g", 0, 0, 512), ("x", 1, 0, 512), ("g", 1, 0, 512), ("g", 2, 0, 512),
-    ("x", 2, 0, 128), ("x", 2, 128, 128), ("x", 2, 256, 128), ("x", 2, 384, 128),
+    ("x", 0, 0, 512, 256), ("g", 0, 0, 512, 256), ("x", 1, 0, 512, 256), ("g", 1, 0, 512, 256), ("g", 2, 0, 512, 256),
+    ("x", 2, 0, 128, 64), ("x", 2, 128, 128, 64), ("x", 2, 256, 128, 64), ("x", 2, 384, 128, 64),
 ]
 
 
@@ -52,67 +44,56 @@ def tile_linear_kernel(tc, x, w0, w1, w2, grad_out, out):
 
         sources = {"x": x, "g": grad_out}
         formats = {"x": E4M3X4, "g": E5M2X4}
-        codes = {}
-        planes = {}
-        for c in range(CHUNKS):
-            for i in range(DIM):
-                codes[("g", c, i)] = mx_pool.tile([P, MUL], U32, name="gc_%d_%d" % (c, i), align_bytes=64)
-                planes[("g", c, i)] = mx_pool.tile([P, MUL], U8, name="gs_%d_%d" % (c, i), align_bytes=64)
         acc = [psum.tile([P, MUL], F32, name="acc%d" % m) for m in range(M_TILES)]
 
         warm = res_pool.tile([P, 8], F32, name="warm")
         nc.vector.memset(warm[:], 0.0)
         nc.scalar.mul(warm[:], warm[:], 1.0)
 
-        raw = {}
-        for (o, c, u0, width) in LOADS:
+        raw = []
+        for (o, c, u0, width, v_share) in LOADS:
             t = raw_pool.tile([P, PACK, DIM * width], BF16, name="raw_%s%d_%d" % (o, c, u0))
             rows = sources[o][c * K_PASS:(c + 1) * K_PASS, OFF + DIM * u0:OFF + DIM * (u0 + width)]
             nc.sync.dma_start(out=t[:], in_=rows.rearrange("(p j) w -> p j w", j=PACK))
-            for (oo, cc, uu, ww, vv) in PIECES:
-                if oo == o and cc == c and u0 <= uu and uu + ww <= u0 + width:
-                    raw[(oo, cc, uu)] = (t, uu - u0)
+            raw.append(t)
 
-        def regroup(k):
-            o, c, u0, width, v_share = PIECES[k]
-            g = grp_pool.tile([P, DIM, width, PACK], BF16, name="grp_%d" % k, align_bytes=64)
-            t, first = raw[(o, c, u0)]
-            src = t[:].rearrange("p j (u i) -> p u j i", i=DIM)
-            dst = g[:].rearrange("p i u j -> p u j i")
-            nc.vector.tensor_copy(out=dst[:, 0:v_share, :, :], in_=src[:, first:first + v_share, :, :])
-            nc.scalar.copy(out=dst[:, v_share:width, :, :], in_=src[:, first + v_share:first + width, :, :])
-            return g
+        units = [(k, i) for k in range(len(LOADS)) for i in range(DIM)]
+        grouped = {}
+        codes = {}
+        planes = {}
 
-        def quantise(k, g):
-            o, c, u0, width, v_share = PIECES[k]
-            for i in range(DIM):
-                if o == "x":
-                    codes[(o, c, i, u0)] = mx_pool.tile([P, width], U32, name="xc_%d_%d_%d" % (c, i, u0), align_bytes=64)
-                    planes[(o, c, i, u0)] = mx_pool.tile([P, width], U8, name="xs_%d_%d_%d" % (c, i, u0), align_bytes=64)
-                    words = codes[(o, c, i, u0)][:, :]
-                    plane = planes[(o, c, i, u0)][:, :]
-                else:
-                    words = codes[(o, c, i)][:, u0:u0 + width]
-                    plane = planes[(o, c, i)][:, u0:u0 + width]
-                nc.vector.quantize_mx(
-                    out=words.bitcast(formats[o]),
-                    scales=plane,
-                    in_=g[:, i, :, :].rearrange("p u j -> p (u j)"),
-                )
+        def regroup(k, i):
+            o, c, u0, width, v_share = LOADS[k]
+            g = grp_pool.tile([P, width, PACK], BF16, name="grp_%d_%d" % (k, i), align_bytes=64)
+            src = raw[k][:].rearrange("p j (a b i) -> p i a j b", b=RUN, i=DIM)[:, i, :, :, :]
+            dst = g[:].rearrange("p (a b) j -> p a j b", b=RUN)
+            cut = v_share // RUN
+            nc.vector.tensor_copy(out=dst[:, 0:cut, :, :], in_=src[:, 0:cut, :, :])
+            nc.scalar.copy(out=dst[:, cut:, :, :], in_=src[:, cut:, :, :])
+            grouped[(k, i)] = g
 
-        def passes(c, u0, width):
+        def quantise(k, i):
+            o, c, u0, width, v_share = LOADS[k]
+            codes[(o, c, i, u0)] = mx_pool.tile([P, width], U32, name="c%s_%d_%d_%d" % (o, c, i, u0), align_bytes=64)
+            planes[(o, c, i, u0)] = mx_pool.tile([P, width], U8, name="s%s_%d_%d_%d" % (o, c, i, u0), align_bytes=64)
+            nc.vector.quantize_mx(
+                out=codes[(o, c, i, u0)][:, :].bitcast(formats[o]),
+                scales=planes[(o, c, i, u0)][:, :],
+                in_=grouped[(k, i)][:].rearrange("p u j -> p (u j)"),
+            )
+
+        def passes(c, i, u0, width):
             for m in range(u0 // M_TILE, (u0 + width) // M_TILE):
                 cols = slice(m * M_TILE - u0, (m + 1) * M_TILE - u0)
-                for i in range(DIM):
-                    nc.tensor.matmul_mx(
-                        out=acc[m][:],
-                        lhsT=codes[("x", c, i, u0)][:, cols].bitcast(E4M3X4),
-                        lhsT_scale=planes[("x", c, i, u0)][:, cols],
-                        rhs=codes[("g", c, i)][:, :].bitcast(E5M2X4),
-                        rhs_scale=planes[("g", c, i)][:, :],
-                        start=(c == 0 and i == 0),
-                        stop=(c == CHUNKS - 1 and i == DIM - 1),
-                    )
+                nc.tensor.matmul_mx(
+                    out=acc[m][:],
+                    lhsT=codes[("x", c, i, u0)][:, cols].bitcast(E4M3X4),
+                    lhsT_scale=planes[("x", c, i, u0)][:, cols],
+                    rhs=codes[("g", c, i, 0)][:, :].bitcast(E5M2X4),
+                    rhs_scale=planes[("g", c, i, 0)][:, :],
+                    start=(c == 0 and i == 0),
+                    stop=(c == CHUNKS - 1 and i == DIM - 1),
+                )
 
         def finish(m):
             rows = out[m * M_TILE:(m + 1) * M_TILE, :]
@@ -127,26 +108,23 @@ def tile_linear_kernel(tc, x, w0, w1, w2, grad_out, out):
                     nc.vector.tensor_scalar_mul(out=res[:], in0=acc[m][:, h * half:(h + 1) * half], scalar1=scale)
                     nc.sync.dma_start(out=rows[:, h * half:(h + 1) * half], in_=res[:])
 
-        n = len(PIECES)
+        n = len(units)
         waiting = []
-        g_done = {}
-        grouped = {}
-        for k in range(n + 1):
-            if k < n:
-                grouped[k] = regroup(k)
-            if k > 0:
-                o, c, u0, width, v_share = PIECES[k - 1]
-                quantise(k - 1, grouped[k - 1])
-                if o == "g":
-                    g_done[c] = g_done.get(c, 0) + width
-                else:
-                    waiting.append((c, u0, width))
+        for t in range(n + 1):
+            if t < n:
+                regroup(units[t][0], units[t][1])
+            if t > 0:
+                k, i = units[t - 1]
+                o, c, u0, width, v_share = LOADS[k]
+                quantise(k, i)
+                if o == "x":
+                    waiting.append((c, i, u0, width))
                 still = []
-                for (cc, uu, ww) in waiting:
-                    if g_done.get(cc, 0) == MUL:
-                        passes(cc, uu, ww)
+                for (cc, ii, uu, ww) in waiting:
+                    if ("g", cc, ii, 0) in codes:
+                        passes(cc, ii, uu, ww)
                     else:
-                        still.append((cc, uu, ww))
+                        still.append((cc, ii, uu, ww))
                 waiting = still
         for m in range(M_TILES):
             finish(m)

@@ -27,7 +27,7 @@ BYTES = 2 * TOKENS * DIM * MUL * 2 + MUL * MUL * 4
 
 LOADS = [
     ("x", 0, 0, 512, 256), ("g", 0, 0, 512, 256), ("x", 1, 0, 512, 256), ("g", 1, 0, 512, 256), ("g", 2, 0, 512, 256),
-    ("x", 2, 0, 128, 64), ("x", 2, 128, 128, 64), ("x", 2, 256, 128, 64), ("x", 2, 384, 128, 64),
+    ("x", 2, 0, 128, 48), ("x", 2, 128, 128, 48), ("x", 2, 256, 128, 48), ("x", 2, 384, 128, 48),
 ]
 
 
@@ -57,20 +57,27 @@ def tile_linear_kernel(tc, x, w0, w1, w2, grad_out, out):
             nc.sync.dma_start(out=t[:], in_=rows.rearrange("(p j) w -> p j w", j=PACK))
             raw.append(t)
 
-        units = [(k, i) for k in range(len(LOADS)) for i in range(DIM)]
+        steps = []
+        for k in range(len(LOADS)):
+            if LOADS[k][3] == MUL:
+                steps.extend([(k, [i]) for i in range(DIM)])
+            else:
+                steps.append((k, list(range(DIM))))
         grouped = {}
         codes = {}
         planes = {}
 
-        def regroup(k, i):
+        def regroup(k, comps):
             o, c, u0, width, v_share = LOADS[k]
-            g = grp_pool.tile([P, width, PACK], BF16, name="grp_%d_%d" % (k, i), align_bytes=64)
-            src = raw[k][:].rearrange("p j (a b i) -> p i a j b", b=RUN, i=DIM)[:, i, :, :, :]
-            dst = g[:].rearrange("p (a b) j -> p a j b", b=RUN)
+            n = len(comps)
+            g = grp_pool.tile([P, n, width, PACK], BF16, name="grp_%d_%d" % (k, comps[0]), align_bytes=64)
+            src = raw[k][:].rearrange("p j (a b i) -> p a i j b", b=RUN, i=DIM)[:, :, comps[0]:comps[0] + n, :, :]
+            dst = g[:].rearrange("p i (a b) j -> p a i j b", b=RUN)
             cut = v_share // RUN
-            nc.vector.tensor_copy(out=dst[:, 0:cut, :, :], in_=src[:, 0:cut, :, :])
-            nc.scalar.copy(out=dst[:, cut:, :, :], in_=src[:, cut:, :, :])
-            grouped[(k, i)] = g
+            nc.vector.tensor_copy(out=dst[:, 0:cut, :, :, :], in_=src[:, 0:cut, :, :, :])
+            nc.scalar.copy(out=dst[:, cut:, :, :, :], in_=src[:, cut:, :, :, :])
+            for i in comps:
+                grouped[(k, i)] = g[:, i - comps[0], :, :]
 
         def quantise(k, i):
             o, c, u0, width, v_share = LOADS[k]
@@ -79,7 +86,7 @@ def tile_linear_kernel(tc, x, w0, w1, w2, grad_out, out):
             nc.vector.quantize_mx(
                 out=codes[(o, c, i, u0)][:, :].bitcast(formats[o]),
                 scales=planes[(o, c, i, u0)][:, :],
-                in_=grouped[(k, i)][:].rearrange("p u j -> p (u j)"),
+                in_=grouped[(k, i)].rearrange("p u j -> p (u j)"),
             )
 
         def passes(c, i, u0, width):
@@ -108,23 +115,24 @@ def tile_linear_kernel(tc, x, w0, w1, w2, grad_out, out):
                     nc.vector.tensor_scalar_mul(out=res[:], in0=acc[m][:, h * half:(h + 1) * half], scalar1=scale)
                     nc.sync.dma_start(out=rows[:, h * half:(h + 1) * half], in_=res[:])
 
-        n = len(units)
+        n = len(steps)
         waiting = []
         for t in range(n + 1):
             if t < n:
-                regroup(units[t][0], units[t][1])
+                regroup(steps[t][0], steps[t][1])
             if t > 0:
-                k, i = units[t - 1]
+                k, comps = steps[t - 1]
                 o, c, u0, width, v_share = LOADS[k]
-                quantise(k, i)
-                if o == "x":
-                    waiting.append((c, i, u0, width))
-                still = []
-                for (cc, ii, uu, ww) in waiting:
-                    if ("g", cc, ii, 0) in codes:
-                        passes(cc, ii, uu, ww)
-                    else:
-                        still.append((cc, ii, uu, ww))
-                waiting = still
+                for i in comps:
+                    quantise(k, i)
+                    if o == "x":
+                        waiting.append((c, i, u0, width))
+                    still = []
+                    for (cc, ii, uu, ww) in waiting:
+                        if ("g", cc, ii, 0) in codes:
+                            passes(cc, ii, uu, ww)
+                        else:
+                            still.append((cc, ii, uu, ww))
+                    waiting = still
         for m in range(M_TILES):
             finish(m)

@@ -26,7 +26,8 @@ FLOPS = 2 * DIM * TOKENS * MUL * MUL
 BYTES = 2 * TOKENS * DIM * MUL * 2 + MUL * MUL * 4
 
 LOADS = [
-    ("x", 0, 0, 512, 256), ("g", 0, 0, 512, 256), ("x", 1, 0, 512, 256), ("g", 1, 0, 512, 256), ("g", 2, 0, 512, 256),
+    ("x", 0, 0, 512, 256), ("g", 0, 0, 512, 256), ("x", 1, 0, 512, 256),
+    ("g", 1, 0, 256, 128), ("g", 1, 256, 256, 128), ("g", 2, 0, 256, 128), ("g", 2, 256, 256, 128),
     ("x", 2, 0, 128, 48), ("x", 2, 128, 128, 48), ("x", 2, 256, 128, 48), ("x", 2, 384, 128, 48),
 ]
 
@@ -66,6 +67,7 @@ def tile_linear_kernel(tc, x, w0, w1, w2, grad_out, out):
         grouped = {}
         codes = {}
         planes = {}
+        made = {}
 
         def regroup(k, comps):
             o, c, u0, width, v_share = LOADS[k]
@@ -81,23 +83,26 @@ def tile_linear_kernel(tc, x, w0, w1, w2, grad_out, out):
 
         def quantise(k, i):
             o, c, u0, width, v_share = LOADS[k]
-            codes[(o, c, i, u0)] = mx_pool.tile([P, width], U32, name="c%s_%d_%d_%d" % (o, c, i, u0), align_bytes=64)
-            planes[(o, c, i, u0)] = mx_pool.tile([P, width], U8, name="s%s_%d_%d_%d" % (o, c, i, u0), align_bytes=64)
+            if (o, c, i) not in codes:
+                codes[(o, c, i)] = mx_pool.tile([P, MUL], U32, name="c%s_%d_%d" % (o, c, i), align_bytes=64)
+                planes[(o, c, i)] = mx_pool.tile([P, MUL], U8, name="s%s_%d_%d" % (o, c, i), align_bytes=64)
+                made[(o, c, i)] = 0
             nc.vector.quantize_mx(
-                out=codes[(o, c, i, u0)][:, :].bitcast(formats[o]),
-                scales=planes[(o, c, i, u0)][:, :],
+                out=codes[(o, c, i)][:, u0:u0 + width].bitcast(formats[o]),
+                scales=planes[(o, c, i)][:, u0:u0 + width],
                 in_=grouped[(k, i)].rearrange("p u j -> p (u j)"),
             )
+            made[(o, c, i)] = made[(o, c, i)] + width
 
         def passes(c, i, u0, width):
             for m in range(u0 // M_TILE, (u0 + width) // M_TILE):
-                cols = slice(m * M_TILE - u0, (m + 1) * M_TILE - u0)
+                cols = slice(m * M_TILE, (m + 1) * M_TILE)
                 nc.tensor.matmul_mx(
                     out=acc[m][:],
-                    lhsT=codes[("x", c, i, u0)][:, cols].bitcast(E4M3X4),
-                    lhsT_scale=planes[("x", c, i, u0)][:, cols],
-                    rhs=codes[("g", c, i, 0)][:, :].bitcast(E5M2X4),
-                    rhs_scale=planes[("g", c, i, 0)][:, :],
+                    lhsT=codes[("x", c, i)][:, cols].bitcast(E4M3X4),
+                    lhsT_scale=planes[("x", c, i)][:, cols],
+                    rhs=codes[("g", c, i)][:, :].bitcast(E5M2X4),
+                    rhs_scale=planes[("g", c, i)][:, :],
                     start=(c == 0 and i == 0),
                     stop=(c == CHUNKS - 1 and i == DIM - 1),
                 )
@@ -129,7 +134,7 @@ def tile_linear_kernel(tc, x, w0, w1, w2, grad_out, out):
                         waiting.append((c, i, u0, width))
                     still = []
                     for (cc, ii, uu, ww) in waiting:
-                        if ("g", cc, ii, 0) in codes:
+                        if made.get(("g", cc, ii), 0) == MUL:
                             passes(cc, ii, uu, ww)
                         else:
                             still.append((cc, ii, uu, ww))

from contextlib import ExitStack
import math

import concourse.mybir as mybir

BF16 = mybir.dt.bfloat16
F32 = mybir.dt.float32
U32 = mybir.dt.uint32
U8 = mybir.dt.uint8
E4M3X4 = mybir.dt.float8_e4m3fn_x4
E5M2X4 = mybir.dt.float8_e5m2_x4

P = 128
PACK = 4
K_PASS = P * PACK
TOKENS = 1536
MUL = 512
DIM = 3
OFF = 512
CHUNKS = TOKENS // K_PASS
M_TILE = 128
M_TILES = MUL // M_TILE
RUN = 8

FLOPS = 2 * DIM * TOKENS * MUL * MUL
BYTES = 2 * TOKENS * DIM * MUL * 2 + MUL * MUL * 4

LOADS = [
    ("x", 0, 0, 512, 256), ("g", 0, 0, 512, 256), ("x", 1, 0, 512, 256),
    ("g", 1, 0, 256, 128), ("g", 1, 256, 256, 128), ("g", 2, 0, 256, 128), ("g", 2, 256, 256, 128),
    ("x", 2, 0, 128, 48), ("x", 2, 128, 128, 48), ("x", 2, 256, 128, 48), ("x", 2, 384, 128, 48),
]


def tile_linear_kernel(tc, x, w0, w1, w2, grad_out, out):
    nc = tc.nc
    scale = 1.0 / math.sqrt(MUL)
    with ExitStack() as ctx:
        raw_pool = ctx.enter_context(tc.tile_pool(name="raw", bufs=1))
        grp_pool = ctx.enter_context(tc.tile_pool(name="grp", bufs=1))
        mx_pool = ctx.enter_context(tc.tile_pool(name="mx", bufs=1))
        res_pool = ctx.enter_context(tc.tile_pool(name="res", bufs=1))
        psum = ctx.enter_context(tc.psum_pool(name="acc", bufs=1))
        ctx.enter_context(tc.manual_schedule())

        sources = {"x": x, "g": grad_out}
        formats = {"x": E4M3X4, "g": E5M2X4}
        acc = [psum.tile([P, MUL], F32, name="acc%d" % m) for m in range(M_TILES)]

        warm = res_pool.tile([P, 8], F32, name="warm")
        nc.vector.memset(warm[:], 0.0)
        nc.scalar.mul(warm[:], warm[:], 1.0)

        raw = []
        for (o, c, u0, width, v_share) in LOADS:
            t = raw_pool.tile([P, PACK, DIM * width], BF16, name="raw_%s%d_%d" % (o, c, u0))
            rows = sources[o][c * K_PASS:(c + 1) * K_PASS, OFF + DIM * u0:OFF + DIM * (u0 + width)]
            nc.sync.dma_start(out=t[:], in_=rows.rearrange("(p j) w -> p j w", j=PACK))
            raw.append(t)

        steps = []
        for k in range(len(LOADS)):
            if LOADS[k][3] == MUL:
                steps.extend([(k, [i]) for i in range(DIM)])
            else:
                steps.append((k, list(range(DIM))))
        grouped = {}
        codes = {}
        planes = {}
        made = {}

        def regroup(k, comps):
            o, c, u0, width, v_share = LOADS[k]
            n = len(comps)
            g = grp_pool.tile([P, n, width, PACK], BF16, name="grp_%d_%d" % (k, comps[0]), align_bytes=64)
            src = raw[k][:].rearrange("p j (a b i) -> p a i j b", b=RUN, i=DIM)[:, :, comps[0]:comps[0] + n, :, :]
            dst = g[:].rearrange("p i (a b) j -> p a i j b", b=RUN)
            cut = v_share // RUN
            nc.vector.tensor_copy(out=dst[:, 0:cut, :, :, :], in_=src[:, 0:cut, :, :, :])
            nc.scalar.copy(out=dst[:, cut:, :, :, :], in_=src[:, cut:, :, :, :])
            for i in comps:
                grouped[(k, i)] = g[:, i - comps[0], :, :]

        def quantise(k, i):
            o, c, u0, width, v_share = LOADS[k]
            if (o, c, i) not in codes:
                codes[(o, c, i)] = mx_pool.tile([P, MUL], U32, name="c%s_%d_%d" % (o, c, i), align_bytes=64)
                planes[(o, c, i)] = mx_pool.tile([P, MUL], U8, name="s%s_%d_%d" % (o, c, i), align_bytes=64)
                made[(o, c, i)] = 0
            nc.vector.quantize_mx(
                out=codes[(o, c, i)][:, u0:u0 + width].bitcast(formats[o]),
                scales=planes[(o, c, i)][:, u0:u0 + width],
                in_=grouped[(k, i)].rearrange("p u j -> p (u j)"),
            )
            made[(o, c, i)] = made[(o, c, i)] + width

        def passes(c, i, u0, width):
            for m in range(u0 // M_TILE, (u0 + width) // M_TILE):
                cols = slice(m * M_TILE, (m + 1) * M_TILE)
                nc.tensor.matmul_mx(
                    out=acc[m][:],
                    lhsT=codes[("x", c, i)][:, cols].bitcast(E4M3X4),
                    lhsT_scale=planes[("x", c, i)][:, cols],
                    rhs=codes[("g", c, i)][:, :].bitcast(E5M2X4),
                    rhs_scale=planes[("g", c, i)][:, :],
                    start=(c == 0 and i == 0),
                    stop=(c == CHUNKS - 1 and i == DIM - 1),
                )

        def finish(m):
            rows = out[m * M_TILE:(m + 1) * M_TILE, :]
            if m < M_TILES - 1:
                res = res_pool.tile([P, MUL], F32, name="res%d" % m)
                nc.scalar.mul(res[:], acc[m][:], scale)
                nc.sync.dma_start(out=rows, in_=res[:])
            else:
                half = MUL // 2
                for h in range(2):
                    res = res_pool.tile([P, half], F32, name="res%d_%d" % (m, h))
                    nc.vector.tensor_scalar_mul(out=res[:], in0=acc[m][:, h * half:(h + 1) * half], scalar1=scale)
                    nc.sync.dma_start(out=rows[:, h * half:(h + 1) * half], in_=res[:])

        n = len(steps)
        waiting = []
        for t in range(n + 1):
            if t < n:
                regroup(steps[t][0], steps[t][1])
            if t > 0:
                k, comps = steps[t - 1]
                o, c, u0, width, v_share = LOADS[k]
                for i in comps:
                    quantise(k, i)
                    if o == "x":
                        waiting.append((c, i, u0, width))
                    still = []
                    for (cc, ii, uu, ww) in waiting:
                        if made.get(("g", cc, ii), 0) == MUL:
                            passes(cc, ii, uu, ww)
                        else:
                            still.append((cc, ii, uu, ww))
                    waiting = still
        for m in range(M_TILES):
            finish(m)
